import numpy as np
import ml_dtypes


def mxq(x, axis, fmt="e4m3"):
    dtype, down = {"e4m3": (ml_dtypes.float8_e4m3fn, 7), "e5m2": (ml_dtypes.float8_e5m2, 14)}[fmt]
    v = np.moveaxis(np.asarray(x, np.float32).astype(ml_dtypes.bfloat16).astype(np.float64), axis, -1)
    blocks = v.reshape(v.shape[:-1] + (-1, 32))
    amax = np.abs(blocks).max(-1, keepdims=True)
    byte = np.maximum(np.where(amax > 0, np.frexp(amax)[1] - 1 + 127, 0) - down, 1)
    scale = np.exp2(byte - 127.0)
    codes = (blocks / scale).astype(np.float32).astype(dtype).astype(np.float64)
    return np.moveaxis((codes * scale).reshape(v.shape), -1, axis)


WIDE = False


def mx_kscale(k):
    if not WIDE:
        return np.ones(k)
    levels = np.array([10, -10, 5, -5, 0])
    if k % 512:
        return np.exp2(np.random.permutation(np.resize(levels, k // 32))).repeat(32)
    a = np.empty((k // 512, 16))
    for p in range(k // 512):
        a[p, :8] = np.random.permutation(np.resize(levels, 8))
        for g in range(8):
            far = levels[np.abs(levels - a[p, g]) >= 10]
            a[p, g + 8] = far[np.random.randint(len(far))]
    return np.exp2(a.ravel()).repeat(32)


BF16 = ml_dtypes.bfloat16


def bf(x):
    return np.asarray(x, np.float32).astype(BF16)


def f64(x):
    return np.asarray(x).astype(np.float64)


SIZE, DIM, FDIM = 8192, 1024, 128
EPS = 1e-5


def setup_inputs():
    s = mx_kscale(DIM)
    r = np.random.uniform(0.4, 2.0, (SIZE, 1))
    g = np.random.standard_normal((SIZE, DIM))
    return {"lt_weight": bf(g * s / np.sqrt(np.sum(s * s)) * r),
            "Lambdas": bf(np.random.standard_normal((DIM, FDIM)) * 1.5 * np.sqrt(np.mean(s * s)) / s[:, None]),
            "bias": bf(np.random.uniform(0.0, 2.0 * np.pi, FDIM))}


def reference(lt_weight, Lambdas, bias):
    x = f64(lt_weight)
    norms = np.linalg.norm(x, axis=-1, keepdims=True)
    maxnorm = 1.0 - EPS
    e_all = x * np.minimum(1.0, maxnorm / np.maximum(norms, EPS))
    scale = np.sqrt(2.0) / np.sqrt(DIM)
    return scale * np.cos((mxq(e_all, 1, "e4m3") @ mxq(f64(Lambdas), 0, "e4m3")) + f64(bias))

@@ -1,0 +1,284 @@
+import math
+from contextlib import ExitStack
+
+import concourse.mybir as mybir
+from concourse.masks import make_identity
+
+BF16 = mybir.dt.bfloat16
+F32 = mybir.dt.float32
+I32 = mybir.dt.int32
+U32 = mybir.dt.uint32
+U8 = mybir.dt.uint8
+FP8X4 = mybir.dt.float8_e4m3fn_x4
+ALU = mybir.AluOpType
+ACT = mybir.ActivationFunctionType
+
+SIZE, DIM, FDIM = 8192, 1024, 128
+EPS = 1e-5
+P = 128
+BLOCKS = 4
+TILES = SIZE // (P * BLOCKS)
+N_BLOCKS = TILES * BLOCKS
+PASSES = DIM // 512
+WORDS = DIM // 2
+MAGIC = 12582912.0
+FLOPS = 2 * SIZE * DIM * FDIM
+WIDTH = BLOCKS * FDIM
+PREFETCH = 7
+SQUARES_AHEAD = 10
+CLAMP_AHEAD = 4
+SCALE_AHEAD = 2
+SCALAR_FROM = 6
+
+
+def tile_rff_t_kernel(tc, lt_weight, Lambdas, bias, out):
+    nc = tc.nc
+    x_view = lt_weight.rearrange("(a p j) k -> a p j k", p=P, j=BLOCKS)
+    out_view = out.rearrange("(a p j) f -> a p (j f)", p=P, j=BLOCKS)
+    with ExitStack() as ctx:
+        const = ctx.enter_context(tc.tile_pool(name="const", bufs=1))
+        xpool = ctx.enter_context(tc.tile_pool(name="xpool", bufs=TILES))
+        work = ctx.enter_context(tc.tile_pool(name="work", bufs=2))
+        epool = ctx.enter_context(tc.tile_pool(name="epool", bufs=4))
+        small = ctx.enter_context(tc.tile_pool(name="small", bufs=6))
+        psum_t = ctx.enter_context(tc.psum_pool(name="psum_t", bufs=4))
+        psum_z = ctx.enter_context(tc.psum_pool(name="psum_z", bufs=2))
+        psum_f = ctx.enter_context(tc.psum_pool(name="psum_f", bufs=1))
+        ctx.enter_context(tc.manual_schedule())
+
+        xs = []
+
+        def load(a, step):
+            x_sb = xpool.tile([P, BLOCKS, DIM], BF16, name="x_sb")
+            for b in range(0, BLOCKS, step):
+                nc.sync.dma_start(out=x_sb[:, b : b + step, :], in_=x_view[a][:, b : b + step, :])
+            xs.append(x_sb)
+
+        load(0, 1)
+        lam_raw = const.tile([P, PASSES, 4, FDIM], BF16)
+        nc.sync.dma_start(out=lam_raw[:], in_=Lambdas.rearrange("(g p t) n -> p g t n", g=PASSES, p=P, t=4))
+        load(1, 2)
+        bias_bf = const.tile([P, FDIM], BF16)
+        nc.sync.dma_start(out=bias_bf[:], in_=bias.partition_broadcast(P))
+        for a in range(2, PREFETCH):
+            load(a, 4)
+
+        ident = const.tile([P, P], F32)
+        make_identity(nc, ident[:])
+        neg_half = const.tile([P, 4], F32)
+        nc.gpsimd.memset(neg_half[:], -0.5)
+        warm = const.tile([P, 1], F32)
+        nc.vector.memset(warm[:], 0.0)
+        nc.scalar.activation(out=warm[:], in_=warm[:], func=ACT.Sin)
+
+        fill_raw = const.tile([P, 2048], BF16, align_bytes=64)
+        nc.vector.memset(fill_raw[:].bitcast(I32), 0)
+        fill_codes = const.tile([P, 512], U32, align_bytes=64)
+        fill_scales = const.tile([P, 512], U8, align_bytes=64)
+        nc.vector.quantize_mx(out=fill_codes[:].bitcast(FP8X4), scales=fill_scales[:], in_=fill_raw[:])
+        fill_out = psum_f.tile([P, 512], F32)
+
+        def filler():
+            nc.tensor.matmul_mx(
+                out=fill_out[:],
+                lhsT=fill_codes[:, 0:P].bitcast(FP8X4),
+                lhsT_scale=fill_scales[:, 0:P],
+                rhs=fill_codes[:].bitcast(FP8X4),
+                rhs_scale=fill_scales[:],
+                start=True,
+                stop=True,
+            )
+
+        lam_codes = const.tile([P, PASSES * FDIM], U32, align_bytes=64)
+        lam_scales = const.tile([P, PASSES * FDIM], U8, align_bytes=64)
+        turn_bias = const.tile([P, BLOCKS, FDIM], F32)
+
+        def prepare_lambdas():
+            lam_grp = const.tile([P, PASSES, FDIM, 4], BF16, name="lam_grp", align_bytes=64)
+            for g in range(PASSES):
+                nc.vector.tensor_copy(out=lam_grp[:, g, :, :], in_=lam_raw[:, g, :, :].rearrange("p t n -> p n t"))
+            nc.vector.quantize_mx(
+                out=lam_codes[:].bitcast(FP8X4),
+                scales=lam_scales[:],
+                in_=lam_grp[:].rearrange("p g n t -> p (g n t)"),
+            )
+
+        def prepare_bias():
+            for j in range(BLOCKS):
+                nc.vector.tensor_scalar(
+                    out=turn_bias[:, j, :], in0=bias_bf[:], scalar1=1.0 / (2.0 * math.pi), scalar2=0.25,
+                    op0=ALU.mult, op1=ALU.add,
+                )
+
+        state = {}
+
+        def unit_of(blk):
+            if blk < 4:
+                return blk, 1
+            if blk < 8:
+                return blk - blk % 2, 2
+            return blk - blk % 4, 4
+
+        def squares(blk):
+            if not 0 <= blk < N_BLOCKS:
+                return
+            first, count = unit_of(blk)
+            if blk == first:
+                state[("part", first)] = small.tile([P, count], F32, name="part")
+            col = blk - first
+            junk = work.tile([P, DIM], BF16, name="junk")
+            nc.scalar.activation(
+                out=junk[:], in_=xs[blk // BLOCKS][:, blk % BLOCKS, :], func=ACT.Square, scale=1.0 / (1.0 - EPS),
+                accum_out=state[("part", first)][:, col : col + 1],
+            )
+
+        def clamp(blk):
+            if not 0 <= blk < N_BLOCKS or unit_of(blk)[0] != blk:
+                return
+            cols = unit_of(blk)[1]
+            big = small.tile([P, cols], F32, name="big")
+            nc.vector.tensor_scalar(
+                out=big[:], in0=state[("part", blk)][:], scalar1=1.0, scalar2=None, op0=ALU.max
+            )
+            f = small.tile([P, cols], F32, name="f")
+            nc.gpsimd.tensor_tensor(out=f[:], in0=big[:], in1=neg_half[:, 0:cols], op=ALU.pow)
+            state[("f", blk)] = f
+
+        def scale_and_turn(blk):
+            if not 0 <= blk < N_BLOCKS:
+                return
+            t, b = blk // BLOCKS, blk % BLOCKS
+            first = unit_of(blk)[0]
+            f = state[("f", first)]
+            e_sb = epool.tile([P, DIM], BF16, name="e_sb", align_bytes=64)
+            col = blk - first
+            nc.vector.tensor_scalar(
+                out=e_sb[:].rearrange("p (u w e) -> p u w e", u=2, e=2),
+                in0=xs[t][:, b, :].rearrange("p (w u e) -> p u w e", u=2, e=2),
+                scalar1=f[:, col : col + 1], scalar2=None, op0=ALU.mult,
+            )
+            e_t = psum_t.tile([P, 2 * PASSES, P], F32, name="e_t")
+            words = e_sb[:].bitcast(F32)
+            for s in range(2 * PASSES):
+                nc.tensor.transpose(out=e_t[:, s, :], in_=words[:, s * P : (s + 1) * P], identity=ident[:])
+            state[("e_t", blk)] = e_t
+            filler()
+
+        def on_scalar(blk):
+            if blk < SCALAR_FROM:
+                return False
+            if blk >= N_BLOCKS - SQUARES_AHEAD:
+                return blk % 3 != 2
+            return blk % 12 in (1, 4, 6, 9, 11)
+
+        def empty(blk):
+            if not 0 <= blk < N_BLOCKS:
+                return
+            t, b = blk // BLOCKS, blk % BLOCKS
+            if b == 0:
+                state[("grouped", t)] = work.tile([P, BLOCKS, 2 * DIM // 2], BF16, name="grouped", align_bytes=64)
+            copy = nc.scalar.copy if on_scalar(blk) else nc.vector.tensor_copy
+            copy(
+                out=state[("grouped", t)][:, b, :].bitcast(F32).rearrange("p (x u) -> p x u", u=2),
+                in_=state[("e_t", blk)][:].rearrange("p (u g) m -> p (g m) u", u=2),
+            )
+
+        def quantise_and_multiply(blk):
+            if not 0 <= blk < N_BLOCKS:
+                return
+            t, b = blk // BLOCKS, blk % BLOCKS
+            if b == 0:
+                state[("codes", t)] = work.tile([P, BLOCKS * PASSES * P], U32, name="codes", align_bytes=64)
+                state[("scales", t)] = work.tile([P, BLOCKS * PASSES * P], U8, name="scales", align_bytes=64)
+                state[("z", t)] = psum_z.tile([P, WIDTH], F32, name="z")
+            codes, scales, z = state[("codes", t)], state[("scales", t)], state[("z", t)]
+            blk_cols = slice(b * PASSES * P, (b + 1) * PASSES * P)
+            nc.vector.quantize_mx(
+                out=codes[:, blk_cols].bitcast(FP8X4), scales=scales[:, blk_cols], in_=state[("grouped", t)][:, b, :]
+            )
+            for g in range(PASSES):
+                cols = slice((b * PASSES + g) * P, (b * PASSES + g + 1) * P)
+                lam_cols = slice(g * FDIM, (g + 1) * FDIM)
+                nc.tensor.matmul_mx(
+                    out=z[:, b * FDIM : (b + 1) * FDIM],
+                    lhsT=codes[:, cols].bitcast(FP8X4),
+                    lhsT_scale=scales[:, cols],
+                    rhs=lam_codes[:, lam_cols].bitcast(FP8X4),
+                    rhs_scale=lam_scales[:, lam_cols],
+                    start=(g == 0),
+                    stop=(g == PASSES - 1),
+                )
+
+        def tile_of(kind, t, dtype, bufs):
+            if (kind, t) not in state:
+                state[(kind, t)] = work.tile([P, WIDTH], dtype, name=kind, bufs=bufs)
+            return state[(kind, t)]
+
+        def to_turns(t, lo, hi):
+            nc.vector.scalar_tensor_tensor(
+                out=tile_of("turns", t, F32, 2)[:, lo:hi], in0=state[("z", t)][:, lo:hi], scalar=1.0 / (2.0 * math.pi),
+                in1=turn_bias[:].rearrange("p j f -> p (j f)")[:, lo:hi], op0=ALU.mult, op1=ALU.add,
+            )
+
+        def to_whole(t, lo, hi):
+            nc.vector.tensor_scalar(
+                out=tile_of("whole", t, I32, 2)[:, lo:hi], in0=state[("turns", t)][:, lo:hi],
+                scalar1=MAGIC, scalar2=MAGIC, op0=ALU.add, op1=ALU.subtract,
+            )
+
+        def to_frac(t, lo, hi):
+            nc.vector.tensor_tensor(
+                out=tile_of("frac", t, F32, 2)[:, lo:hi], in0=state[("turns", t)][:, lo:hi],
+                in1=state[("whole", t)][:, lo:hi], op=ALU.subtract,
+            )
+
+        def sine(t, lo, hi):
+            nc.scalar.activation(
+                out=tile_of("wave", t, F32, 2)[:, lo:hi], in_=state[("frac", t)][:, lo:hi], func=ACT.Sin,
+                scale=2.0 * math.pi,
+            )
+
+        def finish(t, lo, hi):
+            res = tile_of("res", t, F32, 3)
+            nc.vector.tensor_scalar(
+                out=res[:, lo:hi], in0=state[("wave", t)][:, lo:hi], scalar1=math.sqrt(2.0 / DIM), scalar2=None,
+                op0=ALU.mult,
+            )
+            nc.sync.dma_start(out=out_view[t][:, lo:hi], in_=res[:, lo:hi])
+
+        last = TILES - 1
+        half = WIDTH // 2
+        for blk in range(-SQUARES_AHEAD, N_BLOCKS + 2 * BLOCKS):
+            a, i = blk // BLOCKS, blk % BLOCKS
+            squares(blk + SQUARES_AHEAD)
+            if i == 1 and 0 <= a - 2 < last:
+                sine(a - 2, 0, WIDTH)
+            clamp(blk + CLAMP_AHEAD)
+            scale_and_turn(blk + SCALE_AHEAD)
+            if blk == -1:
+                prepare_lambdas()
+            if blk == 1:
+                prepare_bias()
+            empty(blk)
+            if i == 3 and 0 <= a - 2 < last:
+                finish(a - 2, 0, WIDTH)
+            if i == 3 and a >= 0 and a + PREFETCH < TILES:
+                load(a + PREFETCH, 4)
+            quantise_and_multiply(blk - 1)
+            if i == 1 and 0 <= a - 1 < last:
+                to_turns(a - 1, 0, WIDTH)
+            if i == 2 and 0 <= a - 1 < last:
+                to_whole(a - 1, 0, WIDTH)
+            if i == 3 and 0 <= a - 1 < last:
+                to_frac(a - 1, 0, WIDTH)
+            if blk == N_BLOCKS - 1:
+                to_turns(last, 0, half)
+            if blk == N_BLOCKS:
+                to_whole(last, 0, half)
+                to_frac(last, 0, half)
+                to_turns(last, half, WIDTH)
+                to_whole(last, half, WIDTH)
+                to_frac(last, half, WIDTH)
+        for lo in (0, half):
+            sine(last, lo, lo + half)
+            finish(last, lo, lo + half)

@@ -25,10 +25,13 @@ MAGIC = 12582912.0
 FLOPS = 2 * SIZE * DIM * FDIM
 WIDTH = BLOCKS * FDIM
 PREFETCH = 7
-SQUARES_AHEAD = 10
-CLAMP_AHEAD = 4
+PAIRS = N_BLOCKS // 2
+SQUARES_AHEAD = 5
+CLAMP_AHEAD = 3
 SCALE_AHEAD = 2
 SCALAR_FROM = 6
+VECTOR_SQUARES = (1, 3)
+SCALAR_ALL = N_BLOCKS - 12
 
 
 def tile_rff_t_kernel(tc, lt_weight, Lambdas, bias, out):
@@ -39,11 +42,10 @@ def tile_rff_t_kernel(tc, lt_weight, Lambdas, bias, out):
         const = ctx.enter_context(tc.tile_pool(name="const", bufs=1))
         xpool = ctx.enter_context(tc.tile_pool(name="xpool", bufs=TILES))
         work = ctx.enter_context(tc.tile_pool(name="work", bufs=2))
-        epool = ctx.enter_context(tc.tile_pool(name="epool", bufs=4))
+        epool = ctx.enter_context(tc.tile_pool(name="epool", bufs=6))
         small = ctx.enter_context(tc.tile_pool(name="small", bufs=6))
-        psum_t = ctx.enter_context(tc.psum_pool(name="psum_t", bufs=4))
+        psum_t = ctx.enter_context(tc.psum_pool(name="psum_t", bufs=6))
         psum_z = ctx.enter_context(tc.psum_pool(name="psum_z", bufs=2))
-        psum_f = ctx.enter_context(tc.psum_pool(name="psum_f", bufs=1))
         ctx.enter_context(tc.manual_schedule())
 
         xs = []
@@ -71,24 +73,6 @@ def tile_rff_t_kernel(tc, lt_weight, Lambdas, bias, out):
         nc.vector.memset(warm[:], 0.0)
         nc.scalar.activation(out=warm[:], in_=warm[:], func=ACT.Sin)
 
-        fill_raw = const.tile([P, 2048], BF16, align_bytes=64)
-        nc.vector.memset(fill_raw[:].bitcast(I32), 0)
-        fill_codes = const.tile([P, 512], U32, align_bytes=64)
-        fill_scales = const.tile([P, 512], U8, align_bytes=64)
-        nc.vector.quantize_mx(out=fill_codes[:].bitcast(FP8X4), scales=fill_scales[:], in_=fill_raw[:])
-        fill_out = psum_f.tile([P, 512], F32)
-
-        def filler():
-            nc.tensor.matmul_mx(
-                out=fill_out[:],
-                lhsT=fill_codes[:, 0:P].bitcast(FP8X4),
-                lhsT_scale=fill_scales[:, 0:P],
-                rhs=fill_codes[:].bitcast(FP8X4),
-                rhs_scale=fill_scales[:],
-                start=True,
-                stop=True,
-            )
-
         lam_codes = const.tile([P, PASSES * FDIM], U32, align_bytes=64)
         lam_scales = const.tile([P, PASSES * FDIM], U8, align_bytes=64)
         turn_bias = const.tile([P, BLOCKS, FDIM], F32)
@@ -113,8 +97,6 @@ def tile_rff_t_kernel(tc, lt_weight, Lambdas, bias, out):
         state = {}
 
         def unit_of(blk):
-            if blk < 4:
-                return blk, 1
             if blk < 8:
                 return blk - blk % 2, 2
             return blk - blk % 4, 4
@@ -125,6 +107,8 @@ def tile_rff_t_kernel(tc, lt_weight, Lambdas, bias, out):
             first, count = unit_of(blk)
             if blk == first:
                 state[("part", first)] = small.tile([P, count], F32, name="part")
+            if blk in VECTOR_SQUARES:
+                return
             col = blk - first
             junk = work.tile([P, DIM], BF16, name="junk")
             nc.scalar.activation(
@@ -132,10 +116,23 @@ def tile_rff_t_kernel(tc, lt_weight, Lambdas, bias, out):
                 accum_out=state[("part", first)][:, col : col + 1],
             )
 
+        def vector_squares(blk):
+            first = unit_of(blk)[0]
+            col = blk - first
+            x_blk = xs[blk // BLOCKS][:, blk % BLOCKS, :]
+            vjunk = work.tile([P, DIM], BF16, name="vjunk")
+            nc.vector.scalar_tensor_tensor(
+                out=vjunk[:], in0=x_blk, scalar=1.0 / ((1.0 - EPS) * (1.0 - EPS)), in1=x_blk, op0=ALU.mult, op1=ALU.mult,
+                accum_out=state[("part", first)][:, col : col + 1],
+            )
+
         def clamp(blk):
             if not 0 <= blk < N_BLOCKS or unit_of(blk)[0] != blk:
                 return
             cols = unit_of(blk)[1]
+            for other in range(blk, blk + cols):
+                if other in VECTOR_SQUARES:
+                    vector_squares(other)
             big = small.tile([P, cols], F32, name="big")
             nc.vector.tensor_scalar(
                 out=big[:], in0=state[("part", blk)][:], scalar1=1.0, scalar2=None, op0=ALU.max
@@ -162,52 +159,50 @@ def tile_rff_t_kernel(tc, lt_weight, Lambdas, bias, out):
             for s in range(2 * PASSES):
                 nc.tensor.transpose(out=e_t[:, s, :], in_=words[:, s * P : (s + 1) * P], identity=ident[:])
             state[("e_t", blk)] = e_t
-            filler()
 
         def on_scalar(blk):
             if blk < SCALAR_FROM:
                 return False
-            if blk >= N_BLOCKS - SQUARES_AHEAD:
-                return blk % 3 != 2
-            return blk % 12 in (1, 4, 6, 9, 11)
+            if blk >= SCALAR_ALL:
+                return True
+            return blk % 12 in (1, 5, 7, 11)
 
         def empty(blk):
-            if not 0 <= blk < N_BLOCKS:
-                return
-            t, b = blk // BLOCKS, blk % BLOCKS
+            m, b = blk // 2, blk % 2
             if b == 0:
-                state[("grouped", t)] = work.tile([P, BLOCKS, 2 * DIM // 2], BF16, name="grouped", align_bytes=64)
+                state[("grouped", m)] = work.tile([P, 2, DIM], BF16, name="grouped", align_bytes=64, bufs=3)
             copy = nc.scalar.copy if on_scalar(blk) else nc.vector.tensor_copy
             copy(
-                out=state[("grouped", t)][:, b, :].bitcast(F32).rearrange("p (x u) -> p x u", u=2),
+                out=state[("grouped", m)][:, b, :].bitcast(F32).rearrange("p (x u) -> p x u", u=2),
                 in_=state[("e_t", blk)][:].rearrange("p (u g) m -> p (g m) u", u=2),
             )
 
-        def quantise_and_multiply(blk):
-            if not 0 <= blk < N_BLOCKS:
+        def quantise_and_multiply(m):
+            if not 0 <= m < PAIRS:
                 return
-            t, b = blk // BLOCKS, blk % BLOCKS
-            if b == 0:
-                state[("codes", t)] = work.tile([P, BLOCKS * PASSES * P], U32, name="codes", align_bytes=64)
-                state[("scales", t)] = work.tile([P, BLOCKS * PASSES * P], U8, name="scales", align_bytes=64)
+            t = m // 2
+            codes = work.tile([P, 2 * PASSES * P], U32, name="codes", align_bytes=64, bufs=3)
+            scales = work.tile([P, 2 * PASSES * P], U8, name="scales", align_bytes=64, bufs=3)
+            if m % 2 == 0:
                 state[("z", t)] = psum_z.tile([P, WIDTH], F32, name="z")
-            codes, scales, z = state[("codes", t)], state[("scales", t)], state[("z", t)]
-            blk_cols = slice(b * PASSES * P, (b + 1) * PASSES * P)
+            z = state[("z", t)]
             nc.vector.quantize_mx(
-                out=codes[:, blk_cols].bitcast(FP8X4), scales=scales[:, blk_cols], in_=state[("grouped", t)][:, b, :]
+                out=codes[:].bitcast(FP8X4), scales=scales[:], in_=state[("grouped", m)][:].rearrange("p b k -> p (b k)")
             )
-            for g in range(PASSES):
-                cols = slice((b * PASSES + g) * P, (b * PASSES + g + 1) * P)
-                lam_cols = slice(g * FDIM, (g + 1) * FDIM)
-                nc.tensor.matmul_mx(
-                    out=z[:, b * FDIM : (b + 1) * FDIM],
-                    lhsT=codes[:, cols].bitcast(FP8X4),
-                    lhsT_scale=scales[:, cols],
-                    rhs=lam_codes[:, lam_cols].bitcast(FP8X4),
-                    rhs_scale=lam_scales[:, lam_cols],
-                    start=(g == 0),
-                    stop=(g == PASSES - 1),
-                )
+            for b in range(2):
+                j = 2 * (m % 2) + b
+                for g in range(PASSES):
+                    cols = slice((b * PASSES + g) * P, (b * PASSES + g + 1) * P)
+                    lam_cols = slice(g * FDIM, (g + 1) * FDIM)
+                    nc.tensor.matmul_mx(
+                        out=z[:, j * FDIM : (j + 1) * FDIM],
+                        lhsT=codes[:, cols].bitcast(FP8X4),
+                        lhsT_scale=scales[:, cols],
+                        rhs=lam_codes[:, lam_cols].bitcast(FP8X4),
+                        rhs_scale=lam_scales[:, lam_cols],
+                        start=(g == 0),
+                        stop=(g == PASSES - 1),
+                    )
 
         def tile_of(kind, t, dtype, bufs):
             if (kind, t) not in state:
@@ -238,47 +233,60 @@ def tile_rff_t_kernel(tc, lt_weight, Lambdas, bias, out):
                 scale=2.0 * math.pi,
             )
 
-        def finish(t, lo, hi):
+        def finish(t, lo, hi, on_act):
             res = tile_of("res", t, F32, 3)
-            nc.vector.tensor_scalar(
-                out=res[:, lo:hi], in0=state[("wave", t)][:, lo:hi], scalar1=math.sqrt(2.0 / DIM), scalar2=None,
-                op0=ALU.mult,
-            )
+            if on_act:
+                nc.scalar.mul(out=res[:, lo:hi], in_=state[("wave", t)][:, lo:hi], mul=math.sqrt(2.0 / DIM))
+            else:
+                nc.vector.tensor_scalar(
+                    out=res[:, lo:hi], in0=state[("wave", t)][:, lo:hi], scalar1=math.sqrt(2.0 / DIM), scalar2=None,
+                    op0=ALU.mult,
+                )
             nc.sync.dma_start(out=out_view[t][:, lo:hi], in_=res[:, lo:hi])
 
         last = TILES - 1
         half = WIDTH // 2
-        for blk in range(-SQUARES_AHEAD, N_BLOCKS + 2 * BLOCKS):
-            a, i = blk // BLOCKS, blk % BLOCKS
-            squares(blk + SQUARES_AHEAD)
-            if i == 1 and 0 <= a - 2 < last:
-                sine(a - 2, 0, WIDTH)
-            clamp(blk + CLAMP_AHEAD)
-            scale_and_turn(blk + SCALE_AHEAD)
-            if blk == -1:
+        for m in range(-SQUARES_AHEAD, PAIRS + 4):
+            odd = m % 2 == 1
+            first, second = 2 * m, 2 * m + 1
+            t_turn = (m - 3) // 2
+            t_sine = (m - 5) // 2
+            t_done = (m - 7) // 2
+            t_whole = (m - 4) // 2
+            if odd and 0 <= t_sine < last:
+                sine(t_sine, 0, WIDTH)
+            squares(2 * (m + SQUARES_AHEAD))
+            for blk in (2 * (m + CLAMP_AHEAD), 2 * (m + CLAMP_AHEAD) + 1):
+                clamp(blk)
+            scale_and_turn(2 * (m + SCALE_AHEAD))
+            if not odd and 0 <= t_whole < last:
+                to_whole(t_whole, 0, WIDTH)
+            if odd and 0 <= t_done < last:
+                finish(t_done, 0, WIDTH, t_done >= last - 2)
+            scale_and_turn(2 * (m + SCALE_AHEAD) + 1)
+            if m == -1:
                 prepare_lambdas()
-            if blk == 1:
+            if m == 1:
                 prepare_bias()
-            empty(blk)
-            if i == 3 and 0 <= a - 2 < last:
-                finish(a - 2, 0, WIDTH)
-            if i == 3 and a >= 0 and a + PREFETCH < TILES:
-                load(a + PREFETCH, 4)
-            quantise_and_multiply(blk - 1)
-            if i == 1 and 0 <= a - 1 < last:
-                to_turns(a - 1, 0, WIDTH)
-            if i == 2 and 0 <= a - 1 < last:
-                to_whole(a - 1, 0, WIDTH)
-            if i == 3 and 0 <= a - 1 < last:
-                to_frac(a - 1, 0, WIDTH)
-            if blk == N_BLOCKS - 1:
+            if 0 <= m < PAIRS:
+                empty(first)
+            squares(2 * (m + SQUARES_AHEAD) + 1)
+            if 0 <= m < PAIRS:
+                empty(second)
+            quantise_and_multiply(m - 1)
+            if odd and 0 <= t_turn < last:
+                to_turns(t_turn, 0, WIDTH)
+            if not odd and 0 <= t_whole < last:
+                to_frac(t_whole, 0, WIDTH)
+            if m % 2 == 1 and m >= 0 and m // 2 + PREFETCH < TILES:
+                load(m // 2 + PREFETCH, 4)
+            if m == PAIRS:
                 to_turns(last, 0, half)
-            if blk == N_BLOCKS:
-                to_whole(last, 0, half)
-                to_frac(last, 0, half)
                 to_turns(last, half, WIDTH)
+                to_whole(last, 0, half)
                 to_whole(last, half, WIDTH)
+                to_frac(last, 0, half)
                 to_frac(last, half, WIDTH)
         for lo in (0, half):
             sine(last, lo, lo + half)
-            finish(last, lo, lo + half)
+            finish(last, lo, lo + half, lo == 0)

@@ -26,12 +26,12 @@ FLOPS = 2 * SIZE * DIM * FDIM
 WIDTH = BLOCKS * FDIM
 PREFETCH = 7
 PAIRS = N_BLOCKS // 2
-SQUARES_AHEAD = 5
+SQUARES_AHEAD = 6
 CLAMP_AHEAD = 3
 SCALE_AHEAD = 2
 SCALAR_FROM = 6
 VECTOR_SQUARES = (1, 3)
-SCALAR_ALL = N_BLOCKS - 12
+SCALAR_ALL = N_BLOCKS - 14
 
 
 def tile_rff_t_kernel(tc, lt_weight, Lambdas, bias, out):
@@ -44,8 +44,9 @@ def tile_rff_t_kernel(tc, lt_weight, Lambdas, bias, out):
         work = ctx.enter_context(tc.tile_pool(name="work", bufs=2))
         epool = ctx.enter_context(tc.tile_pool(name="epool", bufs=6))
         small = ctx.enter_context(tc.tile_pool(name="small", bufs=6))
-        psum_t = ctx.enter_context(tc.psum_pool(name="psum_t", bufs=6))
+        psum_t = ctx.enter_context(tc.psum_pool(name="psum_t", bufs=5))
         psum_z = ctx.enter_context(tc.psum_pool(name="psum_z", bufs=2))
+        psum_f = ctx.enter_context(tc.psum_pool(name="psum_f", bufs=1))
         ctx.enter_context(tc.manual_schedule())
 
         xs = []
@@ -73,6 +74,24 @@ def tile_rff_t_kernel(tc, lt_weight, Lambdas, bias, out):
         nc.vector.memset(warm[:], 0.0)
         nc.scalar.activation(out=warm[:], in_=warm[:], func=ACT.Sin)
 
+        fill_raw = const.tile([P, 2048], BF16, align_bytes=64)
+        nc.vector.memset(fill_raw[:].bitcast(I32), 0)
+        fill_codes = const.tile([P, 512], U32, align_bytes=64)
+        fill_scales = const.tile([P, 512], U8, align_bytes=64)
+        nc.vector.quantize_mx(out=fill_codes[:].bitcast(FP8X4), scales=fill_scales[:], in_=fill_raw[:])
+        fill_out = psum_f.tile([P, 512], F32)
+
+        def filler():
+            nc.tensor.matmul_mx(
+                out=fill_out[:],
+                lhsT=fill_codes[:, 0:P].bitcast(FP8X4),
+                lhsT_scale=fill_scales[:, 0:P],
+                rhs=fill_codes[:].bitcast(FP8X4),
+                rhs_scale=fill_scales[:],
+                start=True,
+                stop=True,
+            )
+
         lam_codes = const.tile([P, PASSES * FDIM], U32, align_bytes=64)
         lam_scales = const.tile([P, PASSES * FDIM], U8, align_bytes=64)
         turn_bias = const.tile([P, BLOCKS, FDIM], F32)
@@ -97,7 +116,7 @@ def tile_rff_t_kernel(tc, lt_weight, Lambdas, bias, out):
         state = {}
 
         def unit_of(blk):
-            if blk < 8:
+            if blk < 16:
                 return blk - blk % 2, 2
             return blk - blk % 4, 4
 
@@ -165,7 +184,7 @@ def tile_rff_t_kernel(tc, lt_weight, Lambdas, bias, out):
                 return False
             if blk >= SCALAR_ALL:
                 return True
-            return blk % 12 in (1, 5, 7, 11)
+            return blk % 4 == 1
 
         def empty(blk):
             m, b = blk // 2, blk % 2
@@ -256,14 +275,16 @@ def tile_rff_t_kernel(tc, lt_weight, Lambdas, bias, out):
             if odd and 0 <= t_sine < last:
                 sine(t_sine, 0, WIDTH)
             squares(2 * (m + SQUARES_AHEAD))
-            for blk in (2 * (m + CLAMP_AHEAD), 2 * (m + CLAMP_AHEAD) + 1):
-                clamp(blk)
+            if m < 0:
+                clamp(2 * (m + CLAMP_AHEAD))
             scale_and_turn(2 * (m + SCALE_AHEAD))
             if not odd and 0 <= t_whole < last:
                 to_whole(t_whole, 0, WIDTH)
             if odd and 0 <= t_done < last:
                 finish(t_done, 0, WIDTH, t_done >= last - 2)
             scale_and_turn(2 * (m + SCALE_AHEAD) + 1)
+            if m >= 0:
+                clamp(2 * (m + CLAMP_AHEAD))
             if m == -1:
                 prepare_lambdas()
             if m == 1:
@@ -274,6 +295,9 @@ def tile_rff_t_kernel(tc, lt_weight, Lambdas, bias, out):
             if 0 <= m < PAIRS:
                 empty(second)
             quantise_and_multiply(m - 1)
+            if -SCALE_AHEAD <= m < PAIRS:
+                filler()
+                filler()
             if odd and 0 <= t_turn < last:
                 to_turns(t_turn, 0, WIDTH)
             if not odd and 0 <= t_whole < last:

@@ -29,6 +29,7 @@ PAIRS = N_BLOCKS // 2
 SQUARES_AHEAD = 6
 CLAMP_AHEAD = 3
 SCALE_AHEAD = 2
+QUANTISE_BEHIND = 2
 SCALAR_FROM = 6
 VECTOR_SQUARES = (1, 3)
 SCALAR_ALL = N_BLOCKS - 14
@@ -58,12 +59,18 @@ def tile_rff_t_kernel(tc, lt_weight, Lambdas, bias, out):
             xs.append(x_sb)
 
         load(0, 1)
-        lam_raw = const.tile([P, PASSES, 4, FDIM], BF16)
-        nc.sync.dma_start(out=lam_raw[:], in_=Lambdas.rearrange("(g p t) n -> p g t n", g=PASSES, p=P, t=4))
         load(1, 2)
+        load(2, 4)
+        lam_raw = const.tile([P, PASSES, 4, FDIM], BF16)
+        lam_view = Lambdas.rearrange("(g b u q e) n -> q u b g (e n)", g=PASSES, b=16, u=2, q=8, e=2)
+        for q in range(8):
+            for u in range(2):
+                nc.sync.dma_start(
+                    out=lam_raw[q:P:8, :, 2 * u : 2 * u + 2, :].rearrange("p g e n -> p g (e n)"), in_=lam_view[q, u]
+                )
         bias_bf = const.tile([P, FDIM], BF16)
         nc.sync.dma_start(out=bias_bf[:], in_=bias.partition_broadcast(P))
-        for a in range(2, PREFETCH):
+        for a in range(3, PREFETCH):
             load(a, 4)
 
         ident = const.tile([P, P], F32)
@@ -169,8 +176,8 @@ def tile_rff_t_kernel(tc, lt_weight, Lambdas, bias, out):
             e_sb = epool.tile([P, DIM], BF16, name="e_sb", align_bytes=64)
             col = blk - first
             nc.vector.tensor_scalar(
-                out=e_sb[:].rearrange("p (u w e) -> p u w e", u=2, e=2),
-                in0=xs[t][:, b, :].rearrange("p (w u e) -> p u w e", u=2, e=2),
+                out=e_sb[:].rearrange("p (u w e) -> p u w e", u=2, e=16),
+                in0=xs[t][:, b, :].rearrange("p (w u e) -> p u w e", u=2, e=16),
                 scalar1=f[:, col : col + 1], scalar2=None, op0=ALU.mult,
             )
             e_t = psum_t.tile([P, 2 * PASSES, P], F32, name="e_t")
@@ -189,7 +196,7 @@ def tile_rff_t_kernel(tc, lt_weight, Lambdas, bias, out):
         def empty(blk):
             m, b = blk // 2, blk % 2
             if b == 0:
-                state[("grouped", m)] = work.tile([P, 2, DIM], BF16, name="grouped", align_bytes=64, bufs=3)
+                state[("grouped", m)] = work.tile([P, 2, DIM], BF16, name="grouped", align_bytes=64, bufs=4)
             copy = nc.scalar.copy if on_scalar(blk) else nc.vector.tensor_copy
             copy(
                 out=state[("grouped", m)][:, b, :].bitcast(F32).rearrange("p (x u) -> p x u", u=2),
@@ -265,52 +272,58 @@ def tile_rff_t_kernel(tc, lt_weight, Lambdas, bias, out):
 
         last = TILES - 1
         half = WIDTH // 2
-        for m in range(-SQUARES_AHEAD, PAIRS + 4):
+        for m in range(-SQUARES_AHEAD, PAIRS):
             odd = m % 2 == 1
-            first, second = 2 * m, 2 * m + 1
-            t_turn = (m - 3) // 2
-            t_sine = (m - 5) // 2
+            t_turn = (m - 4) // 2
+            t_sine = (m - 6) // 2
+            t_frac = (m - 5) // 2
             t_done = (m - 7) // 2
-            t_whole = (m - 4) // 2
-            if odd and 0 <= t_sine < last:
+            if not odd and t_sine >= 0:
                 sine(t_sine, 0, WIDTH)
             squares(2 * (m + SQUARES_AHEAD))
             if m < 0:
                 clamp(2 * (m + CLAMP_AHEAD))
+            quantise_and_multiply(m - QUANTISE_BEHIND)
             scale_and_turn(2 * (m + SCALE_AHEAD))
-            if not odd and 0 <= t_whole < last:
-                to_whole(t_whole, 0, WIDTH)
-            if odd and 0 <= t_done < last:
-                finish(t_done, 0, WIDTH, t_done >= last - 2)
             scale_and_turn(2 * (m + SCALE_AHEAD) + 1)
+            if m >= -SCALE_AHEAD:
+                filler()
+                filler()
+            if odd and t_done >= 0:
+                finish(t_done, 0, WIDTH, t_done >= last - 3)
+            if not odd and t_turn >= 0:
+                to_turns(t_turn, 0, WIDTH)
             if m >= 0:
                 clamp(2 * (m + CLAMP_AHEAD))
-            if m == -1:
-                prepare_lambdas()
             if m == 1:
+                prepare_lambdas()
                 prepare_bias()
-            if 0 <= m < PAIRS:
-                empty(first)
+            if m >= 0:
+                empty(2 * m)
             squares(2 * (m + SQUARES_AHEAD) + 1)
-            if 0 <= m < PAIRS:
-                empty(second)
-            quantise_and_multiply(m - 1)
-            if -SCALE_AHEAD <= m < PAIRS:
-                filler()
-                filler()
-            if odd and 0 <= t_turn < last:
-                to_turns(t_turn, 0, WIDTH)
-            if not odd and 0 <= t_whole < last:
-                to_frac(t_whole, 0, WIDTH)
-            if m % 2 == 1 and m >= 0 and m // 2 + PREFETCH < TILES:
+            if m >= 0:
+                empty(2 * m + 1)
+            if not odd and t_turn >= 0:
+                to_whole(t_turn, 0, WIDTH)
+            if odd and t_frac >= 0:
+                to_frac(t_frac, 0, WIDTH)
+            if odd and m >= 0 and m // 2 + PREFETCH < TILES:
                 load(m // 2 + PREFETCH, 4)
-            if m == PAIRS:
-                to_turns(last, 0, half)
-                to_turns(last, half, WIDTH)
-                to_whole(last, 0, half)
-                to_whole(last, half, WIDTH)
-                to_frac(last, 0, half)
-                to_frac(last, half, WIDTH)
+        sine(last - 2, 0, WIDTH)
+        quantise_and_multiply(PAIRS - 2)
+        to_turns(last - 1, 0, WIDTH)
+        quantise_and_multiply(PAIRS - 1)
+        to_whole(last - 1, 0, WIDTH)
+        finish(last - 2, 0, WIDTH, True)
+        to_turns(last, 0, half)
+        to_frac(last - 1, 0, WIDTH)
+        sine(last - 1, 0, WIDTH)
+        to_turns(last, half, WIDTH)
+        to_whole(last, 0, half)
+        to_whole(last, half, WIDTH)
+        to_frac(last, 0, half)
+        finish(last - 1, 0, WIDTH, True)
+        to_frac(last, half, WIDTH)
         for lo in (0, half):
             sine(last, lo, lo + half)
-            finish(last, lo, lo + half, lo == 0)
+            finish(last, lo, lo + half, False)

@@ -26,8 +26,8 @@ FLOPS = 2 * SIZE * DIM * FDIM
 WIDTH = BLOCKS * FDIM
 PREFETCH = 7
 PAIRS = N_BLOCKS // 2
-SQUARES_AHEAD = 6
-CLAMP_AHEAD = 3
+SQUARES_AHEAD = 7
+CLAMP_AHEAD = 4
 SCALE_AHEAD = 2
 QUANTISE_BEHIND = 2
 SCALAR_FROM = 6
@@ -191,7 +191,7 @@ def tile_rff_t_kernel(tc, lt_weight, Lambdas, bias, out):
                 return False
             if blk >= SCALAR_ALL:
                 return True
-            return blk % 4 == 1
+            return blk % 8 == 2
 
         def empty(blk):
             m, b = blk // 2, blk % 2
@@ -255,13 +255,18 @@ def tile_rff_t_kernel(tc, lt_weight, Lambdas, bias, out):
 
         def sine(t, lo, hi):
             nc.scalar.activation(
-                out=tile_of("wave", t, F32, 2)[:, lo:hi], in_=state[("frac", t)][:, lo:hi], func=ACT.Sin,
+                out=tile_of("wave", t, F32, 3)[:, lo:hi], in_=state[("frac", t)][:, lo:hi], func=ACT.Sin,
                 scale=2.0 * math.pi,
             )
 
-        def finish(t, lo, hi, on_act):
-            res = tile_of("res", t, F32, 3)
-            if on_act:
+        def finish(t, lo, hi, engine):
+            res = tile_of("res", t, F32, 4)
+            if engine == "pool":
+                nc.gpsimd.tensor_scalar(
+                    out=res[:, lo:hi], in0=state[("wave", t)][:, lo:hi], scalar1=math.sqrt(2.0 / DIM), scalar2=0.0,
+                    op0=ALU.mult, op1=ALU.add,
+                )
+            elif engine == "scalar":
                 nc.scalar.mul(out=res[:, lo:hi], in_=state[("wave", t)][:, lo:hi], mul=math.sqrt(2.0 / DIM))
             else:
                 nc.vector.tensor_scalar(
@@ -277,24 +282,21 @@ def tile_rff_t_kernel(tc, lt_weight, Lambdas, bias, out):
             t_turn = (m - 4) // 2
             t_sine = (m - 6) // 2
             t_frac = (m - 5) // 2
-            t_done = (m - 7) // 2
+            t_done = (m - 8) // 2
             if not odd and t_sine >= 0:
                 sine(t_sine, 0, WIDTH)
             squares(2 * (m + SQUARES_AHEAD))
-            if m < 0:
-                clamp(2 * (m + CLAMP_AHEAD))
             quantise_and_multiply(m - QUANTISE_BEHIND)
             scale_and_turn(2 * (m + SCALE_AHEAD))
             scale_and_turn(2 * (m + SCALE_AHEAD) + 1)
             if m >= -SCALE_AHEAD:
                 filler()
                 filler()
-            if odd and t_done >= 0:
-                finish(t_done, 0, WIDTH, t_done >= last - 3)
+            clamp(2 * (m + CLAMP_AHEAD))
+            if not odd and t_done >= 0:
+                finish(t_done, 0, WIDTH, "pool")
             if not odd and t_turn >= 0:
                 to_turns(t_turn, 0, WIDTH)
-            if m >= 0:
-                clamp(2 * (m + CLAMP_AHEAD))
             if m == 1:
                 prepare_lambdas()
                 prepare_bias()
@@ -309,12 +311,13 @@ def tile_rff_t_kernel(tc, lt_weight, Lambdas, bias, out):
                 to_frac(t_frac, 0, WIDTH)
             if odd and m >= 0 and m // 2 + PREFETCH < TILES:
                 load(m // 2 + PREFETCH, 4)
+        finish(last - 3, 0, WIDTH, "scalar")
         sine(last - 2, 0, WIDTH)
         quantise_and_multiply(PAIRS - 2)
         to_turns(last - 1, 0, WIDTH)
         quantise_and_multiply(PAIRS - 1)
         to_whole(last - 1, 0, WIDTH)
-        finish(last - 2, 0, WIDTH, True)
+        finish(last - 2, 0, WIDTH, "scalar")
         to_turns(last, 0, half)
         to_frac(last - 1, 0, WIDTH)
         sine(last - 1, 0, WIDTH)
@@ -322,8 +325,8 @@ def tile_rff_t_kernel(tc, lt_weight, Lambdas, bias, out):
         to_whole(last, 0, half)
         to_whole(last, half, WIDTH)
         to_frac(last, 0, half)
-        finish(last - 1, 0, WIDTH, True)
+        finish(last - 1, 0, WIDTH, "scalar")
         to_frac(last, half, WIDTH)
         for lo in (0, half):
             sine(last, lo, lo + half)
-            finish(last, lo, lo + half, False)
+            finish(last, lo, lo + half, "vector")

@@ -31,7 +31,7 @@ CLAMP_AHEAD = 4
 SCALE_AHEAD = 2
 QUANTISE_BEHIND = 2
 SCALAR_FROM = 6
-VECTOR_SQUARES = (1, 3)
+VECTOR_SQUARES = (1, 3, 5, 7)
 SCALAR_ALL = N_BLOCKS - 14
 
 
@@ -43,8 +43,8 @@ def tile_rff_t_kernel(tc, lt_weight, Lambdas, bias, out):
         const = ctx.enter_context(tc.tile_pool(name="const", bufs=1))
         xpool = ctx.enter_context(tc.tile_pool(name="xpool", bufs=TILES))
         work = ctx.enter_context(tc.tile_pool(name="work", bufs=2))
-        epool = ctx.enter_context(tc.tile_pool(name="epool", bufs=6))
-        small = ctx.enter_context(tc.tile_pool(name="small", bufs=6))
+        epool = ctx.enter_context(tc.tile_pool(name="epool", bufs=8))
+        small = ctx.enter_context(tc.tile_pool(name="small", bufs=12))
         psum_t = ctx.enter_context(tc.psum_pool(name="psum_t", bufs=5))
         psum_z = ctx.enter_context(tc.psum_pool(name="psum_z", bufs=2))
         psum_f = ctx.enter_context(tc.psum_pool(name="psum_f", bufs=1))
@@ -59,8 +59,9 @@ def tile_rff_t_kernel(tc, lt_weight, Lambdas, bias, out):
             xs.append(x_sb)
 
         load(0, 1)
-        load(1, 2)
-        load(2, 4)
+        load(1, 1)
+        load(2, 1)
+        load(3, 4)
         lam_raw = const.tile([P, PASSES, 4, FDIM], BF16)
         lam_view = Lambdas.rearrange("(g b u q e) n -> q u b g (e n)", g=PASSES, b=16, u=2, q=8, e=2)
         for q in range(8):
@@ -70,7 +71,7 @@ def tile_rff_t_kernel(tc, lt_weight, Lambdas, bias, out):
                 )
         bias_bf = const.tile([P, FDIM], BF16)
         nc.sync.dma_start(out=bias_bf[:], in_=bias.partition_broadcast(P))
-        for a in range(3, PREFETCH):
+        for a in range(4, PREFETCH):
             load(a, 4)
 
         ident = const.tile([P, P], F32)
@@ -136,7 +137,7 @@ def tile_rff_t_kernel(tc, lt_weight, Lambdas, bias, out):
             if blk in VECTOR_SQUARES:
                 return
             col = blk - first
-            junk = work.tile([P, DIM], BF16, name="junk")
+            junk = work.tile([P, DIM], BF16, name="junk", bufs=4)
             nc.scalar.activation(
                 out=junk[:], in_=xs[blk // BLOCKS][:, blk % BLOCKS, :], func=ACT.Square, scale=1.0 / (1.0 - EPS),
                 accum_out=state[("part", first)][:, col : col + 1],
@@ -191,12 +192,12 @@ def tile_rff_t_kernel(tc, lt_weight, Lambdas, bias, out):
                 return False
             if blk >= SCALAR_ALL:
                 return True
-            return blk % 8 == 2
+            return blk % 4 == 2
 
         def empty(blk):
             m, b = blk // 2, blk % 2
             if b == 0:
-                state[("grouped", m)] = work.tile([P, 2, DIM], BF16, name="grouped", align_bytes=64, bufs=4)
+                state[("grouped", m)] = work.tile([P, 2, DIM], BF16, name="grouped", align_bytes=64, bufs=5)
             copy = nc.scalar.copy if on_scalar(blk) else nc.vector.tensor_copy
             copy(
                 out=state[("grouped", m)][:, b, :].bitcast(F32).rearrange("p (x u) -> p x u", u=2),
@@ -207,8 +208,8 @@ def tile_rff_t_kernel(tc, lt_weight, Lambdas, bias, out):
             if not 0 <= m < PAIRS:
                 return
             t = m // 2
-            codes = work.tile([P, 2 * PASSES * P], U32, name="codes", align_bytes=64, bufs=3)
-            scales = work.tile([P, 2 * PASSES * P], U8, name="scales", align_bytes=64, bufs=3)
+            codes = work.tile([P, 2 * PASSES * P], U32, name="codes", align_bytes=64, bufs=4)
+            scales = work.tile([P, 2 * PASSES * P], U8, name="scales", align_bytes=64, bufs=4)
             if m % 2 == 0:
                 state[("z", t)] = psum_z.tile([P, WIDTH], F32, name="z")
             z = state[("z", t)]
@@ -237,19 +238,19 @@ def tile_rff_t_kernel(tc, lt_weight, Lambdas, bias, out):
 
         def to_turns(t, lo, hi):
             nc.vector.scalar_tensor_tensor(
-                out=tile_of("turns", t, F32, 2)[:, lo:hi], in0=state[("z", t)][:, lo:hi], scalar=1.0 / (2.0 * math.pi),
+                out=tile_of("turns", t, F32, 3)[:, lo:hi], in0=state[("z", t)][:, lo:hi], scalar=1.0 / (2.0 * math.pi),
                 in1=turn_bias[:].rearrange("p j f -> p (j f)")[:, lo:hi], op0=ALU.mult, op1=ALU.add,
             )
 
         def to_whole(t, lo, hi):
             nc.vector.tensor_scalar(
-                out=tile_of("whole", t, I32, 2)[:, lo:hi], in0=state[("turns", t)][:, lo:hi],
+                out=tile_of("whole", t, I32, 3)[:, lo:hi], in0=state[("turns", t)][:, lo:hi],
                 scalar1=MAGIC, scalar2=MAGIC, op0=ALU.add, op1=ALU.subtract,
             )
 
         def to_frac(t, lo, hi):
             nc.vector.tensor_tensor(
-                out=tile_of("frac", t, F32, 2)[:, lo:hi], in0=state[("turns", t)][:, lo:hi],
+                out=tile_of("frac", t, F32, 3)[:, lo:hi], in0=state[("turns", t)][:, lo:hi],
                 in1=state[("whole", t)][:, lo:hi], op=ALU.subtract,
             )
 
@@ -286,6 +287,9 @@ def tile_rff_t_kernel(tc, lt_weight, Lambdas, bias, out):
             if not odd and t_sine >= 0:
                 sine(t_sine, 0, WIDTH)
             squares(2 * (m + SQUARES_AHEAD))
+            if m == QUANTISE_BEHIND:
+                prepare_lambdas()
+                prepare_bias()
             quantise_and_multiply(m - QUANTISE_BEHIND)
             scale_and_turn(2 * (m + SCALE_AHEAD))
             scale_and_turn(2 * (m + SCALE_AHEAD) + 1)
@@ -297,9 +301,6 @@ def tile_rff_t_kernel(tc, lt_weight, Lambdas, bias, out):
                 finish(t_done, 0, WIDTH, "pool")
             if not odd and t_turn >= 0:
                 to_turns(t_turn, 0, WIDTH)
-            if m == 1:
-                prepare_lambdas()
-                prepare_bias()
             if m >= 0:
                 empty(2 * m)
             squares(2 * (m + SQUARES_AHEAD) + 1)

@@ -31,6 +31,7 @@ CLAMP_AHEAD = 4
 SCALE_AHEAD = 2
 QUANTISE_BEHIND = 2
 SCALAR_FROM = 6
+SCALAR_SCALES = (N_BLOCKS - 3, N_BLOCKS - 1)
 VECTOR_SQUARES = (1, 3, 5, 7)
 SCALAR_ALL = N_BLOCKS - 14
 
@@ -176,11 +177,14 @@ def tile_rff_t_kernel(tc, lt_weight, Lambdas, bias, out):
             f = state[("f", first)]
             e_sb = epool.tile([P, DIM], BF16, name="e_sb", align_bytes=64)
             col = blk - first
-            nc.vector.tensor_scalar(
-                out=e_sb[:].rearrange("p (u w e) -> p u w e", u=2, e=16),
-                in0=xs[t][:, b, :].rearrange("p (w u e) -> p u w e", u=2, e=16),
-                scalar1=f[:, col : col + 1], scalar2=None, op0=ALU.mult,
-            )
+            e_view = e_sb[:].rearrange("p (u w e) -> p u w e", u=2, e=16)
+            x_perm = xs[t][:, b, :].rearrange("p (w u e) -> p u w e", u=2, e=16)
+            if blk in SCALAR_SCALES:
+                nc.scalar.activation(out=e_view, in_=x_perm, func=ACT.Copy, scale=f[:, col : col + 1])
+            else:
+                nc.vector.tensor_scalar(
+                    out=e_view, in0=x_perm, scalar1=f[:, col : col + 1], scalar2=None, op0=ALU.mult
+                )
             e_t = psum_t.tile([P, 2 * PASSES, P], F32, name="e_t")
             words = e_sb[:].bitcast(F32)
             for s in range(2 * PASSES):
@@ -284,8 +288,6 @@ def tile_rff_t_kernel(tc, lt_weight, Lambdas, bias, out):
             t_sine = (m - 6) // 2
             t_frac = (m - 5) // 2
             t_done = (m - 8) // 2
-            if not odd and t_sine >= 0:
-                sine(t_sine, 0, WIDTH)
             squares(2 * (m + SQUARES_AHEAD))
             if m == QUANTISE_BEHIND:
                 prepare_lambdas()
@@ -295,7 +297,8 @@ def tile_rff_t_kernel(tc, lt_weight, Lambdas, bias, out):
             scale_and_turn(2 * (m + SCALE_AHEAD) + 1)
             if m >= -SCALE_AHEAD:
                 filler()
-                filler()
+                if 2 * m < SCALAR_ALL:
+                    filler()
             clamp(2 * (m + CLAMP_AHEAD))
             if not odd and t_done >= 0:
                 finish(t_done, 0, WIDTH, "pool")
@@ -306,6 +309,8 @@ def tile_rff_t_kernel(tc, lt_weight, Lambdas, bias, out):
             squares(2 * (m + SQUARES_AHEAD) + 1)
             if m >= 0:
                 empty(2 * m + 1)
+            if not odd and t_sine >= 0:
+                sine(t_sine, 0, WIDTH)
             if not odd and t_turn >= 0:
                 to_whole(t_turn, 0, WIDTH)
             if odd and t_frac >= 0:
@@ -317,17 +322,18 @@ def tile_rff_t_kernel(tc, lt_weight, Lambdas, bias, out):
         quantise_and_multiply(PAIRS - 2)
         to_turns(last - 1, 0, WIDTH)
         quantise_and_multiply(PAIRS - 1)
-        to_whole(last - 1, 0, WIDTH)
         finish(last - 2, 0, WIDTH, "scalar")
+        to_whole(last - 1, 0, WIDTH)
         to_turns(last, 0, half)
         to_frac(last - 1, 0, WIDTH)
         sine(last - 1, 0, WIDTH)
-        to_turns(last, half, WIDTH)
         to_whole(last, 0, half)
-        to_whole(last, half, WIDTH)
+        to_turns(last, half, WIDTH)
         to_frac(last, 0, half)
-        finish(last - 1, 0, WIDTH, "scalar")
+        sine(last, 0, half)
+        to_whole(last, half, WIDTH)
         to_frac(last, half, WIDTH)
-        for lo in (0, half):
-            sine(last, lo, lo + half)
-            finish(last, lo, lo + half, "vector")
+        sine(last, half, WIDTH)
+        finish(last - 1, 0, WIDTH, "vector")
+        finish(last, 0, half, "vector")
+        finish(last, half, WIDTH, "vector")

@@ -293,12 +293,14 @@ def tile_rff_t_kernel(tc, lt_weight, Lambdas, bias, out):
                 prepare_lambdas()
                 prepare_bias()
             quantise_and_multiply(m - QUANTISE_BEHIND)
+            if 0 <= 2 * m < SCALAR_ALL:
+                filler()
             scale_and_turn(2 * (m + SCALE_AHEAD))
+            if -SCALE_AHEAD <= m and 2 * m < SCALAR_ALL:
+                filler()
             scale_and_turn(2 * (m + SCALE_AHEAD) + 1)
             if m >= -SCALE_AHEAD:
                 filler()
-                if 2 * m < SCALAR_ALL:
-                    filler()
             clamp(2 * (m + CLAMP_AHEAD))
             if not odd and t_done >= 0:
                 finish(t_done, 0, WIDTH, "pool")

import math
from contextlib import ExitStack

import concourse.mybir as mybir
from concourse.masks import make_identity

BF16 = mybir.dt.bfloat16
F32 = mybir.dt.float32
I32 = mybir.dt.int32
U32 = mybir.dt.uint32
U8 = mybir.dt.uint8
FP8X4 = mybir.dt.float8_e4m3fn_x4
ALU = mybir.AluOpType
ACT = mybir.ActivationFunctionType

SIZE, DIM, FDIM = 8192, 1024, 128
EPS = 1e-5
P = 128
BLOCKS = 4
TILES = SIZE // (P * BLOCKS)
N_BLOCKS = TILES * BLOCKS
PASSES = DIM // 512
WORDS = DIM // 2
MAGIC = 12582912.0
FLOPS = 2 * SIZE * DIM * FDIM
WIDTH = BLOCKS * FDIM
PREFETCH = 7
PAIRS = N_BLOCKS // 2
SQUARES_AHEAD = 7
CLAMP_AHEAD = 4
SCALE_AHEAD = 2
QUANTISE_BEHIND = 2
SCALAR_FROM = 6
SCALAR_SCALES = (N_BLOCKS - 3, N_BLOCKS - 1)
VECTOR_SQUARES = (1, 3, 5, 7)
SCALAR_ALL = N_BLOCKS - 14


def tile_rff_t_kernel(tc, lt_weight, Lambdas, bias, out):
    nc = tc.nc
    x_view = lt_weight.rearrange("(a p j) k -> a p j k", p=P, j=BLOCKS)
    out_view = out.rearrange("(a p j) f -> a p (j f)", p=P, j=BLOCKS)
    with ExitStack() as ctx:
        const = ctx.enter_context(tc.tile_pool(name="const", bufs=1))
        xpool = ctx.enter_context(tc.tile_pool(name="xpool", bufs=TILES))
        work = ctx.enter_context(tc.tile_pool(name="work", bufs=2))
        epool = ctx.enter_context(tc.tile_pool(name="epool", bufs=8))
        small = ctx.enter_context(tc.tile_pool(name="small", bufs=12))
        psum_t = ctx.enter_context(tc.psum_pool(name="psum_t", bufs=5))
        psum_z = ctx.enter_context(tc.psum_pool(name="psum_z", bufs=2))
        psum_f = ctx.enter_context(tc.psum_pool(name="psum_f", bufs=1))
        ctx.enter_context(tc.manual_schedule())

        xs = []

        def load(a, step):
            x_sb = xpool.tile([P, BLOCKS, DIM], BF16, name="x_sb")
            for b in range(0, BLOCKS, step):
                nc.sync.dma_start(out=x_sb[:, b : b + step, :], in_=x_view[a][:, b : b + step, :])
            xs.append(x_sb)

        load(0, 1)
        load(1, 1)
        load(2, 1)
        load(3, 4)
        lam_raw = const.tile([P, PASSES, 4, FDIM], BF16)
        lam_view = Lambdas.rearrange("(g b u q e) n -> q u b g (e n)", g=PASSES, b=16, u=2, q=8, e=2)
        for q in range(8):
            for u in range(2):
                nc.sync.dma_start(
                    out=lam_raw[q:P:8, :, 2 * u : 2 * u + 2, :].rearrange("p g e n -> p g (e n)"), in_=lam_view[q, u]
                )
        bias_bf = const.tile([P, FDIM], BF16)
        nc.sync.dma_start(out=bias_bf[:], in_=bias.partition_broadcast(P))
        for a in range(4, PREFETCH):
            load(a, 4)

        ident = const.tile([P, P], F32)
        make_identity(nc, ident[:])
        neg_half = const.tile([P, 4], F32)
        nc.gpsimd.memset(neg_half[:], -0.5)
        warm = const.tile([P, 1], F32)
        nc.vector.memset(warm[:], 0.0)
        nc.scalar.activation(out=warm[:], in_=warm[:], func=ACT.Sin)

        fill_raw = const.tile([P, 2048], BF16, align_bytes=64)
        nc.vector.memset(fill_raw[:].bitcast(I32), 0)
        fill_codes = const.tile([P, 512], U32, align_bytes=64)
        fill_scales = const.tile([P, 512], U8, align_bytes=64)
        nc.vector.quantize_mx(out=fill_codes[:].bitcast(FP8X4), scales=fill_scales[:], in_=fill_raw[:])
        fill_out = psum_f.tile([P, 512], F32)

        def filler():
            nc.tensor.matmul_mx(
                out=fill_out[:],
                lhsT=fill_codes[:, 0:P].bitcast(FP8X4),
                lhsT_scale=fill_scales[:, 0:P],
                rhs=fill_codes[:].bitcast(FP8X4),
                rhs_scale=fill_scales[:],
                start=True,
                stop=True,
            )

        lam_codes = const.tile([P, PASSES * FDIM], U32, align_bytes=64)
        lam_scales = const.tile([P, PASSES * FDIM], U8, align_bytes=64)
        turn_bias = const.tile([P, BLOCKS, FDIM], F32)

        def prepare_lambdas():
            lam_grp = const.tile([P, PASSES, FDIM, 4], BF16, name="lam_grp", align_bytes=64)
            for g in range(PASSES):
                nc.vector.tensor_copy(out=lam_grp[:, g, :, :], in_=lam_raw[:, g, :, :].rearrange("p t n -> p n t"))
            nc.vector.quantize_mx(
                out=lam_codes[:].bitcast(FP8X4),
                scales=lam_scales[:],
                in_=lam_grp[:].rearrange("p g n t -> p (g n t)"),
            )

        def prepare_bias():
            for j in range(BLOCKS):
                nc.vector.tensor_scalar(
                    out=turn_bias[:, j, :], in0=bias_bf[:], scalar1=1.0 / (2.0 * math.pi), scalar2=0.25,
                    op0=ALU.mult, op1=ALU.add,
                )

        state = {}

        def unit_of(blk):
            if blk < 16:
                return blk - blk % 2, 2
            return blk - blk % 4, 4

        def squares(blk):
            if not 0 <= blk < N_BLOCKS:
                return
            first, count = unit_of(blk)
            if blk == first:
                state[("part", first)] = small.tile([P, count], F32, name="part")
            if blk in VECTOR_SQUARES:
                return
            col = blk - first
            junk = work.tile([P, DIM], BF16, name="junk", bufs=4)
            nc.scalar.activation(
                out=junk[:], in_=xs[blk // BLOCKS][:, blk % BLOCKS, :], func=ACT.Square, scale=1.0 / (1.0 - EPS),
                accum_out=state[("part", first)][:, col : col + 1],
            )

        def vector_squares(blk):
            first = unit_of(blk)[0]
            col = blk - first
            x_blk = xs[blk // BLOCKS][:, blk % BLOCKS, :]
            vjunk = work.tile([P, DIM], BF16, name="vjunk")
            nc.vector.scalar_tensor_tensor(
                out=vjunk[:], in0=x_blk, scalar=1.0 / ((1.0 - EPS) * (1.0 - EPS)), in1=x_blk, op0=ALU.mult, op1=ALU.mult,
                accum_out=state[("part", first)][:, col : col + 1],
            )

        def clamp(blk):
            if not 0 <= blk < N_BLOCKS or unit_of(blk)[0] != blk:
                return
            cols = unit_of(blk)[1]
            for other in range(blk, blk + cols):
                if other in VECTOR_SQUARES:
                    vector_squares(other)
            big = small.tile([P, cols], F32, name="big")
            nc.vector.tensor_scalar(
                out=big[:], in0=state[("part", blk)][:], scalar1=1.0, scalar2=None, op0=ALU.max
            )
            f = small.tile([P, cols], F32, name="f")
            nc.gpsimd.tensor_tensor(out=f[:], in0=big[:], in1=neg_half[:, 0:cols], op=ALU.pow)
            state[("f", blk)] = f

        def scale_and_turn(blk):
            if not 0 <= blk < N_BLOCKS:
                return
            t, b = blk // BLOCKS, blk % BLOCKS
            first = unit_of(blk)[0]
            f = state[("f", first)]
            e_sb = epool.tile([P, DIM], BF16, name="e_sb", align_bytes=64)
            col = blk - first
            e_view = e_sb[:].rearrange("p (u w e) -> p u w e", u=2, e=16)
            x_perm = xs[t][:, b, :].rearrange("p (w u e) -> p u w e", u=2, e=16)
            if blk in SCALAR_SCALES:
                nc.scalar.activation(out=e_view, in_=x_perm, func=ACT.Copy, scale=f[:, col : col + 1])
            else:
                nc.vector.tensor_scalar(
                    out=e_view, in0=x_perm, scalar1=f[:, col : col + 1], scalar2=None, op0=ALU.mult
                )
            e_t = psum_t.tile([P, 2 * PASSES, P], F32, name="e_t")
            words = e_sb[:].bitcast(F32)
            for s in range(2 * PASSES):
                nc.tensor.transpose(out=e_t[:, s, :], in_=words[:, s * P : (s + 1) * P], identity=ident[:])
            state[("e_t", blk)] = e_t

        def on_scalar(blk):
            if blk < SCALAR_FROM:
                return False
            if blk >= SCALAR_ALL:
                return True
            return blk % 4 == 2

        def empty(blk):
            m, b = blk // 2, blk % 2
            if b == 0:
                state[("grouped", m)] = work.tile([P, 2, DIM], BF16, name="grouped", align_bytes=64, bufs=5)
            copy = nc.scalar.copy if on_scalar(blk) else nc.vector.tensor_copy
            copy(
                out=state[("grouped", m)][:, b, :].bitcast(F32).rearrange("p (x u) -> p x u", u=2),
                in_=state[("e_t", blk)][:].rearrange("p (u g) m -> p (g m) u", u=2),
            )

        def quantise_and_multiply(m):
            if not 0 <= m < PAIRS:
                return
            t = m // 2
            codes = work.tile([P, 2 * PASSES * P], U32, name="codes", align_bytes=64, bufs=4)
            scales = work.tile([P, 2 * PASSES * P], U8, name="scales", align_bytes=64, bufs=4)
            if m % 2 == 0:
                state[("z", t)] = psum_z.tile([P, WIDTH], F32, name="z")
            z = state[("z", t)]
            nc.vector.quantize_mx(
                out=codes[:].bitcast(FP8X4), scales=scales[:], in_=state[("grouped", m)][:].rearrange("p b k -> p (b k)")
            )
            for b in range(2):
                j = 2 * (m % 2) + b
                for g in range(PASSES):
                    cols = slice((b * PASSES + g) * P, (b * PASSES + g + 1) * P)
                    lam_cols = slice(g * FDIM, (g + 1) * FDIM)
                    nc.tensor.matmul_mx(
                        out=z[:, j * FDIM : (j + 1) * FDIM],
                        lhsT=codes[:, cols].bitcast(FP8X4),
                        lhsT_scale=scales[:, cols],
                        rhs=lam_codes[:, lam_cols].bitcast(FP8X4),
                        rhs_scale=lam_scales[:, lam_cols],
                        start=(g == 0),
                        stop=(g == PASSES - 1),
                    )

        def tile_of(kind, t, dtype, bufs):
            if (kind, t) not in state:
                state[(kind, t)] = work.tile([P, WIDTH], dtype, name=kind, bufs=bufs)
            return state[(kind, t)]

        def to_turns(t, lo, hi):
            nc.vector.scalar_tensor_tensor(
                out=tile_of("turns", t, F32, 3)[:, lo:hi], in0=state[("z", t)][:, lo:hi], scalar=1.0 / (2.0 * math.pi),
                in1=turn_bias[:].rearrange("p j f -> p (j f)")[:, lo:hi], op0=ALU.mult, op1=ALU.add,
            )

        def to_whole(t, lo, hi):
            nc.vector.tensor_scalar(
                out=tile_of("whole", t, I32, 3)[:, lo:hi], in0=state[("turns", t)][:, lo:hi],
                scalar1=MAGIC, scalar2=MAGIC, op0=ALU.add, op1=ALU.subtract,
            )

        def to_frac(t, lo, hi):
            nc.vector.tensor_tensor(
                out=tile_of("frac", t, F32, 3)[:, lo:hi], in0=state[("turns", t)][:, lo:hi],
                in1=state[("whole", t)][:, lo:hi], op=ALU.subtract,
            )

        def sine(t, lo, hi):
            nc.scalar.activation(
                out=tile_of("wave", t, F32, 3)[:, lo:hi], in_=state[("frac", t)][:, lo:hi], func=ACT.Sin,
                scale=2.0 * math.pi,
            )

        def finish(t, lo, hi, engine):
            res = tile_of("res", t, F32, 4)
            if engine == "pool":
                nc.gpsimd.tensor_scalar(
                    out=res[:, lo:hi], in0=state[("wave", t)][:, lo:hi], scalar1=math.sqrt(2.0 / DIM), scalar2=0.0,
                    op0=ALU.mult, op1=ALU.add,
                )
            elif engine == "scalar":
                nc.scalar.mul(out=res[:, lo:hi], in_=state[("wave", t)][:, lo:hi], mul=math.sqrt(2.0 / DIM))
            else:
                nc.vector.tensor_scalar(
                    out=res[:, lo:hi], in0=state[("wave", t)][:, lo:hi], scalar1=math.sqrt(2.0 / DIM), scalar2=None,
                    op0=ALU.mult,
                )
            nc.sync.dma_start(out=out_view[t][:, lo:hi], in_=res[:, lo:hi])

        last = TILES - 1
        half = WIDTH // 2
        for m in range(-SQUARES_AHEAD, PAIRS):
            odd = m % 2 == 1
            t_turn = (m - 4) // 2
            t_sine = (m - 6) // 2
            t_frac = (m - 5) // 2
            t_done = (m - 8) // 2
            squares(2 * (m + SQUARES_AHEAD))
            if m == QUANTISE_BEHIND:
                prepare_lambdas()
                prepare_bias()
            quantise_and_multiply(m - QUANTISE_BEHIND)
            if 0 <= 2 * m < SCALAR_ALL:
                filler()
            scale_and_turn(2 * (m + SCALE_AHEAD))
            if -SCALE_AHEAD <= m and 2 * m < SCALAR_ALL:
                filler()
            scale_and_turn(2 * (m + SCALE_AHEAD) + 1)
            if m >= -SCALE_AHEAD:
                filler()
            clamp(2 * (m + CLAMP_AHEAD))
            if not odd and t_done >= 0:
                finish(t_done, 0, WIDTH, "pool")
            if not odd and t_turn >= 0:
                to_turns(t_turn, 0, WIDTH)
            if m >= 0:
                empty(2 * m)
            squares(2 * (m + SQUARES_AHEAD) + 1)
            if m >= 0:
                empty(2 * m + 1)
            if not odd and t_sine >= 0:
                sine(t_sine, 0, WIDTH)
            if not odd and t_turn >= 0:
                to_whole(t_turn, 0, WIDTH)
            if odd and t_frac >= 0:
                to_frac(t_frac, 0, WIDTH)
            if odd and m >= 0 and m // 2 + PREFETCH < TILES:
                load(m // 2 + PREFETCH, 4)
        finish(last - 3, 0, WIDTH, "scalar")
        sine(last - 2, 0, WIDTH)
        quantise_and_multiply(PAIRS - 2)
        to_turns(last - 1, 0, WIDTH)
        quantise_and_multiply(PAIRS - 1)
        finish(last - 2, 0, WIDTH, "scalar")
        to_whole(last - 1, 0, WIDTH)
        to_turns(last, 0, half)
        to_frac(last - 1, 0, WIDTH)
        sine(last - 1, 0, WIDTH)
        to_whole(last, 0, half)
        to_turns(last, half, WIDTH)
        to_frac(last, 0, half)
        sine(last, 0, half)
        to_whole(last, half, WIDTH)
        to_frac(last, half, WIDTH)
        sine(last, half, WIDTH)
        finish(last - 1, 0, WIDTH, "vector")
        finish(last, 0, half, "vector")
        finish(last, half, WIDTH, "vector")
